import numpy as np
import ml_dtypes


def mxq(x, axis, fmt="e4m3"):
    dtype, down = {"e4m3": (ml_dtypes.float8_e4m3fn, 7), "e5m2": (ml_dtypes.float8_e5m2, 14)}[fmt]
    v = np.moveaxis(np.asarray(x, np.float32).astype(ml_dtypes.bfloat16).astype(np.float64), axis, -1)
    blocks = v.reshape(v.shape[:-1] + (-1, 32))
    amax = np.abs(blocks).max(-1, keepdims=True)
    byte = np.maximum(np.where(amax > 0, np.frexp(amax)[1] - 1 + 127, 0) - down, 1)
    scale = np.exp2(byte - 127.0)
    codes = (blocks / scale).astype(np.float32).astype(dtype).astype(np.float64)
    return np.moveaxis((codes * scale).reshape(v.shape), -1, axis)


WIDE = False


def mx_kscale(k):
    if not WIDE:
        return np.ones(k)
    levels = np.array([10, -10, 5, -5, 0])
    a = np.random.permutation(np.resize(levels, k // 512 * 4)).reshape(k // 512, 4)
    idx = np.arange(k)
    return np.exp2(a[idx // 512, idx % 128 // 32])


BF16 = ml_dtypes.bfloat16


def bf(x):
    return np.asarray(x, np.float32).astype(BF16)


def f64(x):
    return np.asarray(x).astype(np.float64)


B, DIN, H1, H2, N, I, K, O = 1024, 2048, 1024, 512, 32, 16, 256, 16
KO = K * O
SQ_EPS = 1e-8


def squash(t):
    sq = np.sum(t * t, axis=-1, keepdims=True)
    return (sq / (1.0 + sq)) * t / np.sqrt(sq + SQ_EPS)


def setup_inputs():
    amp = np.exp(0.8 * np.random.standard_normal((B, K, 1)))
    t = np.repeat(np.asarray(mx_kscale(KO))[::O], O)
    h = np.exp2(np.round(np.log2(t) / 2))
    c = h / h.max()
    d = np.where(c < 1.0, 0.0625, 1.0)
    return {"s": bf(np.random.standard_normal((B, K, O)) * amp * 1.4 / np.sqrt(O) * c.reshape(K, O)),
            "Wc": bf(np.random.standard_normal((KO, K)) * 6.0 / np.sqrt(KO) * (d / (c * c))[:, None]),
            "bc": bf(np.random.standard_normal(K) * 0.2)}


def reference(s, Wc, bc):
    v = squash(f64(s)).reshape(B, KO)
    return (mxq(v, 1, "e4m3") @ mxq(f64(Wc), 0, "e4m3")) + f64(bc)

@@ -1,0 +1,249 @@
+from contextlib import ExitStack
+
+import concourse.mybir as mybir
+from concourse.masks import make_identity
+
+F32 = mybir.dt.float32
+BF16 = mybir.dt.bfloat16
+U32 = mybir.dt.uint32
+U8 = mybir.dt.uint8
+FP8X4 = mybir.dt.float8_e4m3fn_x4
+ACT = mybir.ActivationFunctionType
+ALU = mybir.AluOpType
+
+P = 128
+PACK = 4
+K_PASS = P * PACK
+
+BATCH = 1024
+CAPS = 256
+CAP_LEN = 16
+K = CAPS * CAP_LEN
+N_OUT = 256
+SQ_EPS = 1e-8
+
+PASSES = K // K_PASS
+BATCH_TILES = BATCH // P
+LANES = P // PACK
+ROW_GROUPS = P // LANES
+RUNS = ROW_GROUPS * PASSES
+CAPS_PER_RUN = P // CAP_LEN
+CAPS_PER_PART = RUNS * CAPS_PER_RUN
+HALF = K // 2
+PIECE_PASSES = 2
+PIECES = PASSES // PIECE_PASSES
+PIECE_CAPS = PIECE_PASSES * CAPS_PER_RUN
+GPSIMD_PIECES = 2
+
+FLOPS = 2 * BATCH * K * N_OUT
+
+
+def tile_capsulenetwork_pc_kernel(tc, s, Wc, bc, out):
+    nc = tc.nc
+
+    s_runs = s.rearrange("b j o -> (b j o)").rearrange(
+        "(n r ig t c) -> n t r ig c", n=BATCH_TILES, r=LANES, ig=RUNS, t=PACK, c=P
+    )
+    wc_rows = Wc.rearrange("(gt p) n -> p gt n", p=P)
+    out_rows = out.rearrange("(n r i) c -> n i r c", r=LANES, i=ROW_GROUPS)
+
+    with ExitStack() as ctx:
+        const = ctx.enter_context(tc.tile_pool(name="const", bufs=1))
+        s_pool = ctx.enter_context(tc.tile_pool(name="s_pool", bufs=BATCH_TILES))
+        sq_pool = ctx.enter_context(tc.tile_pool(name="sq_pool", bufs=4))
+        small = ctx.enter_context(tc.tile_pool(name="small", bufs=3))
+        v_pool = ctx.enter_context(tc.tile_pool(name="v_pool", bufs=2))
+        piece_pool = ctx.enter_context(tc.tile_pool(name="piece_pool", bufs=6))
+        res_pool = ctx.enter_context(tc.tile_pool(name="res_pool", bufs=3))
+        psum_t = ctx.enter_context(tc.psum_pool(name="psum_t", bufs=4))
+        psum_acc = ctx.enter_context(tc.psum_pool(name="psum_acc", bufs=2))
+        ctx.enter_context(tc.manual_schedule())
+
+        eps_col = const.tile([P, 1], F32)
+        nc.vector.memset(eps_col[:], SQ_EPS)
+        warm = const.tile([P, 1], F32)
+        nc.scalar.activation(out=warm[:], in_=eps_col[:], func=ACT.Sqrt)
+        ident = const.tile([P, P], BF16)
+        make_identity(nc, ident[:])
+        bias_rows = const.tile([P, N_OUT], BF16)
+        wc_raw = const.tile([P, PASSES, PACK, N_OUT], BF16)
+        wc_grouped = const.tile([P, PASSES, N_OUT, PACK], BF16, align_bytes=64)
+        wc_codes = const.tile([P, PASSES * N_OUT], U32, align_bytes=64)
+        wc_scales = const.tile([P, PASSES * N_OUT], U8, align_bytes=64)
+
+        s_tiles = []
+        for n in range(BATCH_TILES):
+            s_nat = s_pool.tile([P, K], BF16)
+            for t in range(PACK):
+                nc.sync.dma_start(
+                    out=s_nat[t:P:PACK, :].rearrange("r (ig c) -> r ig c", c=P),
+                    in_=s_runs[n, t],
+                )
+            s_tiles.append(s_nat)
+            if n == 1:
+                nc.sync.dma_start(out=wc_raw[:].rearrange("p g t n -> p (g t) n"), in_=wc_rows)
+                nc.sync.dma_start(out=bias_rows[:], in_=bc.partition_broadcast(P))
+
+        squares = {}
+        q_tiles = {}
+        roots = {}
+        inverses = {}
+        factors = {}
+        v_tiles = {}
+        grouped = {}
+        accs = {}
+
+        def square(n, h):
+            sq = sq_pool.tile([P, HALF], F32)
+            nc.scalar.activation(
+                out=sq[:], in_=s_tiles[n][:, h * HALF : (h + 1) * HALF], func=ACT.Square
+            )
+            squares[(n, h)] = sq
+
+        def reduce_capsules(n):
+            q = small.tile([P, CAPS_PER_PART], F32)
+            for h in range(2):
+                nc.vector.tensor_reduce(
+                    out=q[:, h * (CAPS_PER_PART // 2) : (h + 1) * (CAPS_PER_PART // 2)],
+                    in_=squares[(n, h)][:].rearrange("p (j o) -> p j o", o=CAP_LEN),
+                    axis=mybir.AxisListType.X,
+                    op=ALU.add,
+                )
+            q_tiles[n] = q
+
+        def root(n):
+            u = small.tile([P, CAPS_PER_PART], F32)
+            nc.scalar.activation(out=u[:], in_=q_tiles[n][:], func=ACT.Sqrt, bias=eps_col[:])
+            roots[n] = u
+
+        def invert(n):
+            denom = small.tile([P, CAPS_PER_PART], F32)
+            nc.vector.scalar_tensor_tensor(
+                out=denom[:], in0=q_tiles[n][:], scalar=1.0, in1=roots[n][:],
+                op0=ALU.add, op1=ALU.mult,
+            )
+            inv = small.tile([P, CAPS_PER_PART], F32)
+            nc.vector.reciprocal(out=inv[:], in_=denom[:])
+            inverses[n] = inv
+
+        def make_factor(n):
+            factor = small.tile([P, CAPS_PER_PART], F32)
+            nc.vector.tensor_tensor(
+                out=factor[:], in0=q_tiles[n][:], in1=inverses[n][:], op=ALU.mult
+            )
+            factors[n] = factor
+
+        def multiply(engine, n, piece):
+            if piece == 0:
+                v_nat = v_pool.tile([P, K], BF16)
+                v_tiles[n] = v_nat
+            caps = slice(piece * PIECE_CAPS, (piece + 1) * PIECE_CAPS)
+            s_caps = s_tiles[n][:].rearrange("p (i gj o) -> p i gj o", i=ROW_GROUPS, o=CAP_LEN)
+            v_caps = v_tiles[n][:].rearrange("p (i gj o) -> p i gj o", i=ROW_GROUPS, o=CAP_LEN)
+            f_caps = factors[n][:].rearrange("p (i gj) -> p i gj", i=ROW_GROUPS)
+            engine.tensor_tensor(
+                out=v_caps[:, :, caps, :],
+                in0=s_caps[:, :, caps, :],
+                in1=f_caps[:, :, caps].unsqueeze(3).to_broadcast(
+                    [P, ROW_GROUPS, PIECE_CAPS, CAP_LEN]
+                ),
+                op=ALU.mult,
+            )
+
+        def transpose(n, piece):
+            v_t = psum_t.tile([P, PIECE_PASSES, K_PASS], BF16)
+            for gg in range(PIECE_PASSES):
+                for i in range(ROW_GROUPS):
+                    run = i * PASSES + piece * PIECE_PASSES + gg
+                    nc.tensor.transpose(
+                        v_t[:, gg, i * P : (i + 1) * P],
+                        v_tiles[n][:, run * P : (run + 1) * P],
+                        ident[:],
+                    )
+            v_grouped = piece_pool.tile([P, PIECE_PASSES * K_PASS], BF16, align_bytes=64)
+            nc.scalar.copy(out=v_grouped[:], in_=v_t[:].rearrange("p g w -> p (g w)"))
+            grouped[(n, piece)] = v_grouped
+
+        def quantise_weights():
+            for g in range(PASSES):
+                nc.vector.tensor_copy(
+                    out=wc_grouped[:, g].rearrange("p (c i) t -> p c t i", i=4),
+                    in_=wc_raw[:, g].rearrange("p t (c i) -> p c t i", i=4),
+                )
+            half = PASSES // 2
+            for h in range(2):
+                cols = slice(h * half * N_OUT, (h + 1) * half * N_OUT)
+                nc.vector.quantize_mx(
+                    out=wc_codes[:, cols].bitcast(FP8X4),
+                    scales=wc_scales[:, cols],
+                    in_=wc_grouped[:, h * half : (h + 1) * half].rearrange("p g n t -> p (g n t)"),
+                )
+
+        def quantise_and_contract(n, piece):
+            v_codes = piece_pool.tile([P, PIECE_PASSES * P], U32, align_bytes=64)
+            v_scales = piece_pool.tile([P, PIECE_PASSES * P], U8, align_bytes=64)
+            nc.vector.quantize_mx(
+                out=v_codes[:].bitcast(FP8X4), scales=v_scales[:], in_=grouped[(n, piece)][:]
+            )
+            if piece == 0:
+                acc = psum_acc.tile([P, N_OUT], F32)
+                accs[n] = acc
+            for gg in range(PIECE_PASSES):
+                g = piece * PIECE_PASSES + gg
+                nc.tensor.matmul_mx(
+                    out=accs[n][:],
+                    lhsT=v_codes[:, gg * P : (gg + 1) * P].bitcast(FP8X4),
+                    lhsT_scale=v_scales[:, gg * P : (gg + 1) * P],
+                    rhs=wc_codes[:, g * N_OUT : (g + 1) * N_OUT].bitcast(FP8X4),
+                    rhs_scale=wc_scales[:, g * N_OUT : (g + 1) * N_OUT],
+                    start=(g == 0),
+                    stop=(g == PASSES - 1),
+                )
+
+        def finish(n):
+            res = res_pool.tile([P, N_OUT], F32)
+            nc.vector.tensor_tensor(out=res[:], in0=accs[n][:], in1=bias_rows[:], op=ALU.add)
+            for i in range(ROW_GROUPS):
+                nc.sync.dma_start(out=out_rows[n, i], in_=res[i * LANES : (i + 1) * LANES, :])
+
+        square(0, 0)
+        square(0, 1)
+        for k in range(BATCH_TILES + 2):
+            reducing = k < BATCH_TILES
+            squaring = k + 1 < BATCH_TILES
+            b = k - 1
+            contracting = 0 <= b < BATCH_TILES
+            storing = 0 <= k - 2
+            on_gpsimd = GPSIMD_PIECES if reducing else 0
+
+            if contracting:
+                for piece in range(on_gpsimd):
+                    multiply(nc.gpsimd, b, piece)
+            if squaring:
+                square(k + 1, 0)
+            if reducing:
+                reduce_capsules(k)
+            if contracting:
+                for piece in range(on_gpsimd, PIECES):
+                    multiply(nc.vector, b, piece)
+                transpose(b, 0)
+            if reducing:
+                root(k)
+            if contracting:
+                transpose(b, 1)
+            if squaring:
+                square(k + 1, 1)
+            if contracting:
+                transpose(b, 2)
+                transpose(b, 3)
+            if reducing:
+                invert(k)
+            if b == 0:
+                quantise_weights()
+            if storing:
+                finish(k - 2)
+            if contracting:
+                for piece in range(PIECES):
+                    quantise_and_contract(b, piece)
+            if reducing:
+                make_factor(k)

@@ -33,7 +33,7 @@ HALF = K // 2
 PIECE_PASSES = 2
 PIECES = PASSES // PIECE_PASSES
 PIECE_CAPS = PIECE_PASSES * CAPS_PER_RUN
-GPSIMD_PIECES = 2
+GPSIMD_PIECES = 0
 
 FLOPS = 2 * BATCH * K * N_OUT
 

@@ -33,7 +33,6 @@ HALF = K // 2
 PIECE_PASSES = 2
 PIECES = PASSES // PIECE_PASSES
 PIECE_CAPS = PIECE_PASSES * CAPS_PER_RUN
-GPSIMD_PIECES = 0
 
 FLOPS = 2 * BATCH * K * N_OUT
 
@@ -59,10 +58,10 @@ def tile_capsulenetwork_pc_kernel(tc, s, Wc, bc, out):
         psum_acc = ctx.enter_context(tc.psum_pool(name="psum_acc", bufs=2))
         ctx.enter_context(tc.manual_schedule())
 
-        eps_col = const.tile([P, 1], F32)
-        nc.vector.memset(eps_col[:], SQ_EPS)
+        one_col = const.tile([P, 1], F32)
+        nc.vector.memset(one_col[:], 1.0)
         warm = const.tile([P, 1], F32)
-        nc.scalar.activation(out=warm[:], in_=eps_col[:], func=ACT.Sqrt)
+        nc.scalar.activation(out=warm[:], in_=one_col[:], func=ACT.Abs_reciprocal_sqrt)
         ident = const.tile([P, P], BF16)
         make_identity(nc, ident[:])
         bias_rows = const.tile([P, N_OUT], BF16)
@@ -74,11 +73,14 @@ def tile_capsulenetwork_pc_kernel(tc, s, Wc, bc, out):
         s_tiles = []
         for n in range(BATCH_TILES):
             s_nat = s_pool.tile([P, K], BF16)
-            for t in range(PACK):
-                nc.sync.dma_start(
-                    out=s_nat[t:P:PACK, :].rearrange("r (ig c) -> r ig c", c=P),
-                    in_=s_runs[n, t],
-                )
+            for h in range(2):
+                for t in range(PACK):
+                    nc.sync.dma_start(
+                        out=s_nat[t:P:PACK, h * HALF : (h + 1) * HALF].rearrange(
+                            "r (ig c) -> r ig c", c=P
+                        ),
+                        in_=s_runs[n, t, :, h * (RUNS // 2) : (h + 1) * (RUNS // 2), :],
+                    )
             s_tiles.append(s_nat)
             if n == 1:
                 nc.sync.dma_start(out=wc_raw[:].rearrange("p g t n -> p (g t) n"), in_=wc_rows)
@@ -86,8 +88,9 @@ def tile_capsulenetwork_pc_kernel(tc, s, Wc, bc, out):
 
         squares = {}
         q_tiles = {}
-        roots = {}
-        inverses = {}
+        one_plus_sqs = {}
+        radicands = {}
+        seeds = {}
         factors = {}
         v_tiles = {}
         grouped = {}
@@ -111,29 +114,45 @@ def tile_capsulenetwork_pc_kernel(tc, s, Wc, bc, out):
                 )
             q_tiles[n] = q
 
-        def root(n):
-            u = small.tile([P, CAPS_PER_PART], F32)
-            nc.scalar.activation(out=u[:], in_=q_tiles[n][:], func=ACT.Sqrt, bias=eps_col[:])
-            roots[n] = u
+        def one_plus_squared(n):
+            one_plus_sq = small.tile([P, CAPS_PER_PART], F32)
+            nc.scalar.activation(
+                out=one_plus_sq[:], in_=q_tiles[n][:], func=ACT.Square, bias=one_col[:]
+            )
+            one_plus_sqs[n] = one_plus_sq
 
-        def invert(n):
-            denom = small.tile([P, CAPS_PER_PART], F32)
+        def radicand(n):
+            d = small.tile([P, CAPS_PER_PART], F32)
             nc.vector.scalar_tensor_tensor(
-                out=denom[:], in0=q_tiles[n][:], scalar=1.0, in1=roots[n][:],
+                out=d[:], in0=q_tiles[n][:], scalar=SQ_EPS, in1=one_plus_sqs[n][:],
                 op0=ALU.add, op1=ALU.mult,
             )
-            inv = small.tile([P, CAPS_PER_PART], F32)
-            nc.vector.reciprocal(out=inv[:], in_=denom[:])
-            inverses[n] = inv
+            radicands[n] = d
+
+        def seed(n):
+            y0 = small.tile([P, CAPS_PER_PART], F32)
+            nc.scalar.activation(out=y0[:], in_=radicands[n][:], func=ACT.Abs_reciprocal_sqrt)
+            y0_sq = small.tile([P, CAPS_PER_PART], F32)
+            nc.scalar.activation(out=y0_sq[:], in_=y0[:], func=ACT.Square)
+            seeds[n] = (y0, y0_sq)
 
         def make_factor(n):
+            y0, y0_sq = seeds[n]
+            minus_half_q_y0 = small.tile([P, CAPS_PER_PART], F32)
+            nc.vector.scalar_tensor_tensor(
+                out=minus_half_q_y0[:], in0=q_tiles[n][:], scalar=-0.5, in1=y0[:],
+                op0=ALU.mult, op1=ALU.mult,
+            )
+            d_y0_sq = small.tile([P, CAPS_PER_PART], F32)
+            nc.vector.tensor_tensor(out=d_y0_sq[:], in0=radicands[n][:], in1=y0_sq[:], op=ALU.mult)
             factor = small.tile([P, CAPS_PER_PART], F32)
-            nc.vector.tensor_tensor(
-                out=factor[:], in0=q_tiles[n][:], in1=inverses[n][:], op=ALU.mult
+            nc.vector.scalar_tensor_tensor(
+                out=factor[:], in0=d_y0_sq[:], scalar=3.0, in1=minus_half_q_y0[:],
+                op0=ALU.subtract, op1=ALU.mult,
             )
             factors[n] = factor
 
-        def multiply(engine, n, piece):
+        def multiply(n, piece):
             if piece == 0:
                 v_nat = v_pool.tile([P, K], BF16)
                 v_tiles[n] = v_nat
@@ -141,7 +160,7 @@ def tile_capsulenetwork_pc_kernel(tc, s, Wc, bc, out):
             s_caps = s_tiles[n][:].rearrange("p (i gj o) -> p i gj o", i=ROW_GROUPS, o=CAP_LEN)
             v_caps = v_tiles[n][:].rearrange("p (i gj o) -> p i gj o", i=ROW_GROUPS, o=CAP_LEN)
             f_caps = factors[n][:].rearrange("p (i gj) -> p i gj", i=ROW_GROUPS)
-            engine.tensor_tensor(
+            nc.vector.tensor_tensor(
                 out=v_caps[:, :, caps, :],
                 in0=s_caps[:, :, caps, :],
                 in1=f_caps[:, :, caps].unsqueeze(3).to_broadcast(
@@ -210,40 +229,32 @@ def tile_capsulenetwork_pc_kernel(tc, s, Wc, bc, out):
         square(0, 1)
         for k in range(BATCH_TILES + 2):
             reducing = k < BATCH_TILES
-            squaring = k + 1 < BATCH_TILES
             b = k - 1
             contracting = 0 <= b < BATCH_TILES
-            storing = 0 <= k - 2
-            on_gpsimd = GPSIMD_PIECES if reducing else 0
 
-            if contracting:
-                for piece in range(on_gpsimd):
-                    multiply(nc.gpsimd, b, piece)
-            if squaring:
+            if k + 1 < BATCH_TILES:
                 square(k + 1, 0)
+                square(k + 1, 1)
             if reducing:
                 reduce_capsules(k)
+                one_plus_squared(k)
             if contracting:
-                for piece in range(on_gpsimd, PIECES):
-                    multiply(nc.vector, b, piece)
-                transpose(b, 0)
+                for piece in range(PIECES // 2):
+                    multiply(b, piece)
+                    transpose(b, piece)
             if reducing:
-                root(k)
+                radicand(k)
+                seed(k)
             if contracting:
-                transpose(b, 1)
-            if squaring:
-                square(k + 1, 1)
-            if contracting:
-                transpose(b, 2)
-                transpose(b, 3)
+                for piece in range(PIECES // 2, PIECES):
+                    multiply(b, piece)
+                    transpose(b, piece)
             if reducing:
-                invert(k)
+                make_factor(k)
             if b == 0:
                 quantise_weights()
-            if storing:
+            if k >= 2:
                 finish(k - 2)
             if contracting:
                 for piece in range(PIECES):
                     quantise_and_contract(b, piece)
-            if reducing:
-                make_factor(k)

@@ -30,6 +30,9 @@ RUNS = ROW_GROUPS * PASSES
 CAPS_PER_RUN = P // CAP_LEN
 CAPS_PER_PART = RUNS * CAPS_PER_RUN
 HALF = K // 2
+QUARTERS = 4
+QUARTER = K // QUARTERS
+QUARTER_CAPS = QUARTER // CAP_LEN
 PIECE_PASSES = 2
 PIECES = PASSES // PIECE_PASSES
 PIECE_CAPS = PIECE_PASSES * CAPS_PER_RUN
@@ -49,13 +52,14 @@ def tile_capsulenetwork_pc_kernel(tc, s, Wc, bc, out):
     with ExitStack() as ctx:
         const = ctx.enter_context(tc.tile_pool(name="const", bufs=1))
         s_pool = ctx.enter_context(tc.tile_pool(name="s_pool", bufs=BATCH_TILES))
-        sq_pool = ctx.enter_context(tc.tile_pool(name="sq_pool", bufs=4))
+        sq_pool = ctx.enter_context(tc.tile_pool(name="sq_pool", bufs=3 * QUARTERS))
         small = ctx.enter_context(tc.tile_pool(name="small", bufs=3))
         v_pool = ctx.enter_context(tc.tile_pool(name="v_pool", bufs=2))
         piece_pool = ctx.enter_context(tc.tile_pool(name="piece_pool", bufs=6))
         res_pool = ctx.enter_context(tc.tile_pool(name="res_pool", bufs=3))
         psum_t = ctx.enter_context(tc.psum_pool(name="psum_t", bufs=4))
         psum_acc = ctx.enter_context(tc.psum_pool(name="psum_acc", bufs=2))
+        psum_f = ctx.enter_context(tc.psum_pool(name="psum_f", bufs=2))
         ctx.enter_context(tc.manual_schedule())
 
         one_col = const.tile([P, 1], F32)
@@ -64,6 +68,8 @@ def tile_capsulenetwork_pc_kernel(tc, s, Wc, bc, out):
         nc.scalar.activation(out=warm[:], in_=one_col[:], func=ACT.Abs_reciprocal_sqrt)
         ident = const.tile([P, P], BF16)
         make_identity(nc, ident[:])
+        ident_f32 = const.tile([P, P], F32)
+        make_identity(nc, ident_f32[:])
         bias_rows = const.tile([P, N_OUT], BF16)
         wc_raw = const.tile([P, PASSES, PACK, N_OUT], BF16)
         wc_grouped = const.tile([P, PASSES, N_OUT, PACK], BF16, align_bytes=64)
@@ -96,19 +102,29 @@ def tile_capsulenetwork_pc_kernel(tc, s, Wc, bc, out):
         grouped = {}
         accs = {}
 
-        def square(n, h):
-            sq = sq_pool.tile([P, HALF], F32)
+        def square_and_fold(n, quarter):
+            sq = sq_pool.tile([P, QUARTER], F32)
             nc.scalar.activation(
-                out=sq[:], in_=s_tiles[n][:, h * HALF : (h + 1) * HALF], func=ACT.Square
+                out=sq[:],
+                in_=s_tiles[n][:, quarter * QUARTER : (quarter + 1) * QUARTER],
+                func=ACT.Square,
             )
-            squares[(n, h)] = sq
+            caps = sq[:].rearrange("p (j o) -> p j o", o=CAP_LEN)
+            nc.gpsimd.tensor_tensor(
+                out=caps[:, :, : CAP_LEN // 2],
+                in0=caps[:, :, : CAP_LEN // 2],
+                in1=caps[:, :, CAP_LEN // 2 :],
+                op=ALU.add,
+            )
+            squares[(n, quarter)] = sq
 
         def reduce_capsules(n):
             q = small.tile([P, CAPS_PER_PART], F32)
-            for h in range(2):
+            for quarter in range(QUARTERS):
+                caps = squares[(n, quarter)][:].rearrange("p (j o) -> p j o", o=CAP_LEN)
                 nc.vector.tensor_reduce(
-                    out=q[:, h * (CAPS_PER_PART // 2) : (h + 1) * (CAPS_PER_PART // 2)],
-                    in_=squares[(n, h)][:].rearrange("p (j o) -> p j o", o=CAP_LEN),
+                    out=q[:, quarter * QUARTER_CAPS : (quarter + 1) * QUARTER_CAPS],
+                    in_=caps[:, :, : CAP_LEN // 2],
                     axis=mybir.AxisListType.X,
                     op=ALU.add,
                 )
@@ -150,7 +166,11 @@ def tile_capsulenetwork_pc_kernel(tc, s, Wc, bc, out):
                 out=factor[:], in0=d_y0_sq[:], scalar=3.0, in1=minus_half_q_y0[:],
                 op0=ALU.subtract, op1=ALU.mult,
             )
-            factors[n] = factor
+            factor_ps = psum_f.tile([P, CAPS_PER_PART], F32)
+            nc.tensor.matmul(
+                out=factor_ps[:], lhsT=ident_f32[:], rhs=factor[:], start=True, stop=True
+            )
+            factors[n] = factor_ps
 
         def multiply(n, piece):
             if piece == 0:
@@ -225,36 +245,45 @@ def tile_capsulenetwork_pc_kernel(tc, s, Wc, bc, out):
             for i in range(ROW_GROUPS):
                 nc.sync.dma_start(out=out_rows[n, i], in_=res[i * LANES : (i + 1) * LANES, :])
 
-        square(0, 0)
-        square(0, 1)
+        LEAD = 2
+        for n in range(LEAD):
+            for quarter in range(QUARTERS):
+                square_and_fold(n, quarter)
         for k in range(BATCH_TILES + 2):
+            squaring = k + LEAD < BATCH_TILES
             reducing = k < BATCH_TILES
             b = k - 1
             contracting = 0 <= b < BATCH_TILES
 
-            if k + 1 < BATCH_TILES:
-                square(k + 1, 0)
-                square(k + 1, 1)
+            if squaring:
+                square_and_fold(k + LEAD, 0)
+                square_and_fold(k + LEAD, 1)
             if reducing:
                 reduce_capsules(k)
                 one_plus_squared(k)
+            if squaring:
+                square_and_fold(k + LEAD, 2)
             if contracting:
-                for piece in range(PIECES // 2):
+                for piece in range(PIECES - 1):
                     multiply(b, piece)
                     transpose(b, piece)
+                multiply(b, PIECES - 1)
             if reducing:
                 radicand(k)
                 seed(k)
             if contracting:
-                for piece in range(PIECES // 2, PIECES):
-                    multiply(b, piece)
-                    transpose(b, piece)
-            if reducing:
-                make_factor(k)
+                transpose(b, PIECES - 1)
+            if squaring:
+                square_and_fold(k + LEAD, 3)
             if b == 0:
                 quantise_weights()
             if k >= 2:
                 finish(k - 2)
             if contracting:
-                for piece in range(PIECES):
+                for piece in range(PIECES // 2):
+                    quantise_and_contract(b, piece)
+            if reducing:
+                make_factor(k)
+            if contracting:
+                for piece in range(PIECES // 2, PIECES):
                     quantise_and_contract(b, piece)

@@ -24,18 +24,16 @@ SQ_EPS = 1e-8
 
 PASSES = K // K_PASS
 BATCH_TILES = BATCH // P
-LANES = P // PACK
-ROW_GROUPS = P // LANES
-RUNS = ROW_GROUPS * PASSES
-CAPS_PER_RUN = P // CAP_LEN
-CAPS_PER_PART = RUNS * CAPS_PER_RUN
-HALF = K // 2
+BLOCK_ROWS = P * P // K
+BLOCKS = P // BLOCK_ROWS
+CAPS_PER_PART = K // CAP_LEN
 QUARTERS = 4
 QUARTER = K // QUARTERS
 QUARTER_CAPS = QUARTER // CAP_LEN
-PIECE_PASSES = 2
-PIECES = PASSES // PIECE_PASSES
-PIECE_CAPS = PIECE_PASSES * CAPS_PER_RUN
+QUARTER_BLOCKS = BLOCKS // QUARTERS
+QUARTER_ROWS = P // QUARTERS
+PAIR = 2
+LEAD = 2
 
 FLOPS = 2 * BATCH * K * N_OUT
 
@@ -43,19 +41,18 @@ FLOPS = 2 * BATCH * K * N_OUT
 def tile_capsulenetwork_pc_kernel(tc, s, Wc, bc, out):
     nc = tc.nc
 
-    s_runs = s.rearrange("b j o -> (b j o)").rearrange(
-        "(n r ig t c) -> n t r ig c", n=BATCH_TILES, r=LANES, ig=RUNS, t=PACK, c=P
+    s_blocks = s.rearrange("b j o -> (b j o)").rearrange(
+        "(n f p c) -> n p f c", n=BATCH_TILES, f=BLOCKS, p=P, c=P
     )
-    wc_rows = Wc.rearrange("(gt p) n -> p gt n", p=P)
-    out_rows = out.rearrange("(n r i) c -> n i r c", r=LANES, i=ROW_GROUPS)
+    wc_rows = Wc.rearrange("(gt c) n -> c gt n", c=P)
 
     with ExitStack() as ctx:
         const = ctx.enter_context(tc.tile_pool(name="const", bufs=1))
         s_pool = ctx.enter_context(tc.tile_pool(name="s_pool", bufs=BATCH_TILES))
-        sq_pool = ctx.enter_context(tc.tile_pool(name="sq_pool", bufs=3 * QUARTERS))
+        sq_pool = ctx.enter_context(tc.tile_pool(name="sq_pool", bufs=(LEAD + 1) * QUARTERS))
         small = ctx.enter_context(tc.tile_pool(name="small", bufs=3))
         v_pool = ctx.enter_context(tc.tile_pool(name="v_pool", bufs=2))
-        piece_pool = ctx.enter_context(tc.tile_pool(name="piece_pool", bufs=6))
+        code_pool = ctx.enter_context(tc.tile_pool(name="code_pool", bufs=6))
         res_pool = ctx.enter_context(tc.tile_pool(name="res_pool", bufs=3))
         psum_t = ctx.enter_context(tc.psum_pool(name="psum_t", bufs=4))
         psum_acc = ctx.enter_context(tc.psum_pool(name="psum_acc", bufs=2))
@@ -80,16 +77,14 @@ def tile_capsulenetwork_pc_kernel(tc, s, Wc, bc, out):
         for n in range(BATCH_TILES):
             s_nat = s_pool.tile([P, K], BF16)
             for h in range(2):
-                for t in range(PACK):
-                    nc.sync.dma_start(
-                        out=s_nat[t:P:PACK, h * HALF : (h + 1) * HALF].rearrange(
-                            "r (ig c) -> r ig c", c=P
-                        ),
-                        in_=s_runs[n, t, :, h * (RUNS // 2) : (h + 1) * (RUNS // 2), :],
-                    )
+                blocks = slice(h * (BLOCKS // 2), (h + 1) * (BLOCKS // 2))
+                nc.sync.dma_start(
+                    out=s_nat[:].rearrange("p (f c) -> p f c", c=P)[:, blocks, :],
+                    in_=s_blocks[n, :, blocks, :],
+                )
             s_tiles.append(s_nat)
             if n == 1:
-                nc.sync.dma_start(out=wc_raw[:].rearrange("p g t n -> p (g t) n"), in_=wc_rows)
+                nc.sync.dma_start(out=wc_raw[:].rearrange("c g t n -> c (g t) n"), in_=wc_rows)
                 nc.sync.dma_start(out=bias_rows[:], in_=bc.partition_broadcast(P))
 
         squares = {}
@@ -172,42 +167,42 @@ def tile_capsulenetwork_pc_kernel(tc, s, Wc, bc, out):
             )
             factors[n] = factor_ps
 
-        def multiply(n, piece):
-            if piece == 0:
+        def multiply(n, quarter):
+            if quarter == 0:
                 v_nat = v_pool.tile([P, K], BF16)
                 v_tiles[n] = v_nat
-            caps = slice(piece * PIECE_CAPS, (piece + 1) * PIECE_CAPS)
-            s_caps = s_tiles[n][:].rearrange("p (i gj o) -> p i gj o", i=ROW_GROUPS, o=CAP_LEN)
-            v_caps = v_tiles[n][:].rearrange("p (i gj o) -> p i gj o", i=ROW_GROUPS, o=CAP_LEN)
-            f_caps = factors[n][:].rearrange("p (i gj) -> p i gj", i=ROW_GROUPS)
+            cols = slice(quarter * QUARTER, (quarter + 1) * QUARTER)
+            caps = slice(quarter * QUARTER_CAPS, (quarter + 1) * QUARTER_CAPS)
             nc.vector.tensor_tensor(
-                out=v_caps[:, :, caps, :],
-                in0=s_caps[:, :, caps, :],
-                in1=f_caps[:, :, caps].unsqueeze(3).to_broadcast(
-                    [P, ROW_GROUPS, PIECE_CAPS, CAP_LEN]
-                ),
+                out=v_tiles[n][:, cols].rearrange("p (j o) -> p j o", o=CAP_LEN),
+                in0=s_tiles[n][:, cols].rearrange("p (j o) -> p j o", o=CAP_LEN),
+                in1=factors[n][:, caps].unsqueeze(2).to_broadcast([P, QUARTER_CAPS, CAP_LEN]),
                 op=ALU.mult,
             )
 
-        def transpose(n, piece):
-            v_t = psum_t.tile([P, PIECE_PASSES, K_PASS], BF16)
-            for gg in range(PIECE_PASSES):
-                for i in range(ROW_GROUPS):
-                    run = i * PASSES + piece * PIECE_PASSES + gg
-                    nc.tensor.transpose(
-                        v_t[:, gg, i * P : (i + 1) * P],
-                        v_tiles[n][:, run * P : (run + 1) * P],
-                        ident[:],
-                    )
-            v_grouped = piece_pool.tile([P, PIECE_PASSES * K_PASS], BF16, align_bytes=64)
-            nc.scalar.copy(out=v_grouped[:], in_=v_t[:].rearrange("p g w -> p (g w)"))
-            grouped[(n, piece)] = v_grouped
+        def transpose(n, quarter):
+            v_t = psum_t.tile([P, QUARTER], BF16)
+            for f in range(QUARTER_BLOCKS):
+                block = quarter * QUARTER_BLOCKS + f
+                nc.tensor.transpose(
+                    v_t[:, f * P : (f + 1) * P], v_tiles[n][:, block * P : (block + 1) * P], ident[:]
+                )
+            if quarter == 0:
+                v_grouped = v_pool.tile([P, K], BF16, align_bytes=64)
+                grouped[n] = v_grouped
+            rows = slice(quarter * QUARTER_ROWS, (quarter + 1) * QUARTER_ROWS)
+            nc.scalar.copy(
+                out=grouped[n][:].bitcast(F32).rearrange("c (g r w) -> c g r w", g=PASSES, w=2)[
+                    :, :, rows, :
+                ],
+                in_=v_t[:].bitcast(F32).rearrange("c (r g w) -> c g r w", g=PASSES, w=2),
+            )
 
         def quantise_weights():
             for g in range(PASSES):
                 nc.vector.tensor_copy(
-                    out=wc_grouped[:, g].rearrange("p (c i) t -> p c t i", i=4),
-                    in_=wc_raw[:, g].rearrange("p t (c i) -> p c t i", i=4),
+                    out=wc_grouped[:, g].rearrange("c (m i) t -> c m t i", i=4),
+                    in_=wc_raw[:, g].rearrange("c t (m i) -> c m t i", i=4),
                 )
             half = PASSES // 2
             for h in range(2):
@@ -215,20 +210,22 @@ def tile_capsulenetwork_pc_kernel(tc, s, Wc, bc, out):
                 nc.vector.quantize_mx(
                     out=wc_codes[:, cols].bitcast(FP8X4),
                     scales=wc_scales[:, cols],
-                    in_=wc_grouped[:, h * half : (h + 1) * half].rearrange("p g n t -> p (g n t)"),
+                    in_=wc_grouped[:, h * half : (h + 1) * half].rearrange("c g n t -> c (g n t)"),
                 )
 
-        def quantise_and_contract(n, piece):
-            v_codes = piece_pool.tile([P, PIECE_PASSES * P], U32, align_bytes=64)
-            v_scales = piece_pool.tile([P, PIECE_PASSES * P], U8, align_bytes=64)
+        def quantise_and_contract(n, pair):
+            v_codes = code_pool.tile([P, PAIR * P], U32, align_bytes=64)
+            v_scales = code_pool.tile([P, PAIR * P], U8, align_bytes=64)
             nc.vector.quantize_mx(
-                out=v_codes[:].bitcast(FP8X4), scales=v_scales[:], in_=grouped[(n, piece)][:]
+                out=v_codes[:].bitcast(FP8X4),
+                scales=v_scales[:],
+                in_=grouped[n][:, pair * PAIR * K_PASS : (pair + 1) * PAIR * K_PASS],
             )
-            if piece == 0:
+            if pair == 0:
                 acc = psum_acc.tile([P, N_OUT], F32)
                 accs[n] = acc
-            for gg in range(PIECE_PASSES):
-                g = piece * PIECE_PASSES + gg
+            for gg in range(PAIR):
+                g = pair * PAIR + gg
                 nc.tensor.matmul_mx(
                     out=accs[n][:],
                     lhsT=v_codes[:, gg * P : (gg + 1) * P].bitcast(FP8X4),
@@ -242,10 +239,8 @@ def tile_capsulenetwork_pc_kernel(tc, s, Wc, bc, out):
         def finish(n):
             res = res_pool.tile([P, N_OUT], F32)
             nc.vector.tensor_tensor(out=res[:], in0=accs[n][:], in1=bias_rows[:], op=ALU.add)
-            for i in range(ROW_GROUPS):
-                nc.sync.dma_start(out=out_rows[n, i], in_=res[i * LANES : (i + 1) * LANES, :])
+            nc.sync.dma_start(out=out[n * P : (n + 1) * P, :], in_=res[:])
 
-        LEAD = 2
         for n in range(LEAD):
             for quarter in range(QUARTERS):
                 square_and_fold(n, quarter)
@@ -264,26 +259,23 @@ def tile_capsulenetwork_pc_kernel(tc, s, Wc, bc, out):
             if squaring:
                 square_and_fold(k + LEAD, 2)
             if contracting:
-                for piece in range(PIECES - 1):
-                    multiply(b, piece)
-                    transpose(b, piece)
-                multiply(b, PIECES - 1)
+                for quarter in range(QUARTERS - 1):
+                    multiply(b, quarter)
+                    transpose(b, quarter)
+                multiply(b, QUARTERS - 1)
             if reducing:
                 radicand(k)
                 seed(k)
             if contracting:
-                transpose(b, PIECES - 1)
+                transpose(b, QUARTERS - 1)
             if squaring:
                 square_and_fold(k + LEAD, 3)
             if b == 0:
                 quantise_weights()
             if k >= 2:
                 finish(k - 2)
-            if contracting:
-                for piece in range(PIECES // 2):
-                    quantise_and_contract(b, piece)
             if reducing:
                 make_factor(k)
             if contracting:
-                for piece in range(PIECES // 2, PIECES):
-                    quantise_and_contract(b, piece)
+                for pair in range(PASSES // PAIR):
+                    quantise_and_contract(b, pair)

from contextlib import ExitStack

import concourse.mybir as mybir
from concourse.masks import make_identity

F32 = mybir.dt.float32
BF16 = mybir.dt.bfloat16
U32 = mybir.dt.uint32
U8 = mybir.dt.uint8
FP8X4 = mybir.dt.float8_e4m3fn_x4
ACT = mybir.ActivationFunctionType
ALU = mybir.AluOpType

P = 128
PACK = 4
K_PASS = P * PACK

BATCH = 1024
CAPS = 256
CAP_LEN = 16
K = CAPS * CAP_LEN
N_OUT = 256
SQ_EPS = 1e-8

PASSES = K // K_PASS
BATCH_TILES = BATCH // P
BLOCK_ROWS = P * P // K
BLOCKS = P // BLOCK_ROWS
CAPS_PER_PART = K // CAP_LEN
QUARTERS = 4
QUARTER = K // QUARTERS
QUARTER_CAPS = QUARTER // CAP_LEN
QUARTER_BLOCKS = BLOCKS // QUARTERS
QUARTER_ROWS = P // QUARTERS
PAIR = 2
LEAD = 2

FLOPS = 2 * BATCH * K * N_OUT


def tile_capsulenetwork_pc_kernel(tc, s, Wc, bc, out):
    nc = tc.nc

    s_blocks = s.rearrange("b j o -> (b j o)").rearrange(
        "(n f p c) -> n p f c", n=BATCH_TILES, f=BLOCKS, p=P, c=P
    )
    wc_rows = Wc.rearrange("(gt c) n -> c gt n", c=P)

    with ExitStack() as ctx:
        const = ctx.enter_context(tc.tile_pool(name="const", bufs=1))
        s_pool = ctx.enter_context(tc.tile_pool(name="s_pool", bufs=BATCH_TILES))
        sq_pool = ctx.enter_context(tc.tile_pool(name="sq_pool", bufs=(LEAD + 1) * QUARTERS))
        small = ctx.enter_context(tc.tile_pool(name="small", bufs=3))
        v_pool = ctx.enter_context(tc.tile_pool(name="v_pool", bufs=2))
        code_pool = ctx.enter_context(tc.tile_pool(name="code_pool", bufs=6))
        res_pool = ctx.enter_context(tc.tile_pool(name="res_pool", bufs=3))
        psum_t = ctx.enter_context(tc.psum_pool(name="psum_t", bufs=4))
        psum_acc = ctx.enter_context(tc.psum_pool(name="psum_acc", bufs=2))
        psum_f = ctx.enter_context(tc.psum_pool(name="psum_f", bufs=2))
        ctx.enter_context(tc.manual_schedule())

        one_col = const.tile([P, 1], F32)
        nc.vector.memset(one_col[:], 1.0)
        warm = const.tile([P, 1], F32)
        nc.scalar.activation(out=warm[:], in_=one_col[:], func=ACT.Abs_reciprocal_sqrt)
        ident = const.tile([P, P], BF16)
        make_identity(nc, ident[:])
        ident_f32 = const.tile([P, P], F32)
        make_identity(nc, ident_f32[:])
        bias_rows = const.tile([P, N_OUT], BF16)
        wc_raw = const.tile([P, PASSES, PACK, N_OUT], BF16)
        wc_grouped = const.tile([P, PASSES, N_OUT, PACK], BF16, align_bytes=64)
        wc_codes = const.tile([P, PASSES * N_OUT], U32, align_bytes=64)
        wc_scales = const.tile([P, PASSES * N_OUT], U8, align_bytes=64)

        s_tiles = []
        for n in range(BATCH_TILES):
            s_nat = s_pool.tile([P, K], BF16)
            for h in range(2):
                blocks = slice(h * (BLOCKS // 2), (h + 1) * (BLOCKS // 2))
                nc.sync.dma_start(
                    out=s_nat[:].rearrange("p (f c) -> p f c", c=P)[:, blocks, :],
                    in_=s_blocks[n, :, blocks, :],
                )
            s_tiles.append(s_nat)
            if n == 1:
                nc.sync.dma_start(out=wc_raw[:].rearrange("c g t n -> c (g t) n"), in_=wc_rows)
                nc.sync.dma_start(out=bias_rows[:], in_=bc.partition_broadcast(P))

        squares = {}
        q_tiles = {}
        one_plus_sqs = {}
        radicands = {}
        seeds = {}
        factors = {}
        v_tiles = {}
        grouped = {}
        accs = {}

        def square_and_fold(n, quarter):
            sq = sq_pool.tile([P, QUARTER], F32)
            nc.scalar.activation(
                out=sq[:],
                in_=s_tiles[n][:, quarter * QUARTER : (quarter + 1) * QUARTER],
                func=ACT.Square,
            )
            caps = sq[:].rearrange("p (j o) -> p j o", o=CAP_LEN)
            nc.gpsimd.tensor_tensor(
                out=caps[:, :, : CAP_LEN // 2],
                in0=caps[:, :, : CAP_LEN // 2],
                in1=caps[:, :, CAP_LEN // 2 :],
                op=ALU.add,
            )
            squares[(n, quarter)] = sq

        def reduce_capsules(n):
            q = small.tile([P, CAPS_PER_PART], F32)
            for quarter in range(QUARTERS):
                caps = squares[(n, quarter)][:].rearrange("p (j o) -> p j o", o=CAP_LEN)
                nc.vector.tensor_reduce(
                    out=q[:, quarter * QUARTER_CAPS : (quarter + 1) * QUARTER_CAPS],
                    in_=caps[:, :, : CAP_LEN // 2],
                    axis=mybir.AxisListType.X,
                    op=ALU.add,
                )
            q_tiles[n] = q

        def one_plus_squared(n):
            one_plus_sq = small.tile([P, CAPS_PER_PART], F32)
            nc.scalar.activation(
                out=one_plus_sq[:], in_=q_tiles[n][:], func=ACT.Square, bias=one_col[:]
            )
            one_plus_sqs[n] = one_plus_sq

        def radicand(n):
            d = small.tile([P, CAPS_PER_PART], F32)
            nc.vector.scalar_tensor_tensor(
                out=d[:], in0=q_tiles[n][:], scalar=SQ_EPS, in1=one_plus_sqs[n][:],
                op0=ALU.add, op1=ALU.mult,
            )
            radicands[n] = d

        def seed(n):
            y0 = small.tile([P, CAPS_PER_PART], F32)
            nc.scalar.activation(out=y0[:], in_=radicands[n][:], func=ACT.Abs_reciprocal_sqrt)
            y0_sq = small.tile([P, CAPS_PER_PART], F32)
            nc.scalar.activation(out=y0_sq[:], in_=y0[:], func=ACT.Square)
            seeds[n] = (y0, y0_sq)

        def make_factor(n):
            y0, y0_sq = seeds[n]
            minus_half_q_y0 = small.tile([P, CAPS_PER_PART], F32)
            nc.vector.scalar_tensor_tensor(
                out=minus_half_q_y0[:], in0=q_tiles[n][:], scalar=-0.5, in1=y0[:],
                op0=ALU.mult, op1=ALU.mult,
            )
            d_y0_sq = small.tile([P, CAPS_PER_PART], F32)
            nc.vector.tensor_tensor(out=d_y0_sq[:], in0=radicands[n][:], in1=y0_sq[:], op=ALU.mult)
            factor = small.tile([P, CAPS_PER_PART], F32)
            nc.vector.scalar_tensor_tensor(
                out=factor[:], in0=d_y0_sq[:], scalar=3.0, in1=minus_half_q_y0[:],
                op0=ALU.subtract, op1=ALU.mult,
            )
            factor_ps = psum_f.tile([P, CAPS_PER_PART], F32)
            nc.tensor.matmul(
                out=factor_ps[:], lhsT=ident_f32[:], rhs=factor[:], start=True, stop=True
            )
            factors[n] = factor_ps

        def multiply(n, quarter):
            if quarter == 0:
                v_nat = v_pool.tile([P, K], BF16)
                v_tiles[n] = v_nat
            cols = slice(quarter * QUARTER, (quarter + 1) * QUARTER)
            caps = slice(quarter * QUARTER_CAPS, (quarter + 1) * QUARTER_CAPS)
            nc.vector.tensor_tensor(
                out=v_tiles[n][:, cols].rearrange("p (j o) -> p j o", o=CAP_LEN),
                in0=s_tiles[n][:, cols].rearrange("p (j o) -> p j o", o=CAP_LEN),
                in1=factors[n][:, caps].unsqueeze(2).to_broadcast([P, QUARTER_CAPS, CAP_LEN]),
                op=ALU.mult,
            )

        def transpose(n, quarter):
            v_t = psum_t.tile([P, QUARTER], BF16)
            for f in range(QUARTER_BLOCKS):
                block = quarter * QUARTER_BLOCKS + f
                nc.tensor.transpose(
                    v_t[:, f * P : (f + 1) * P], v_tiles[n][:, block * P : (block + 1) * P], ident[:]
                )
            if quarter == 0:
                v_grouped = v_pool.tile([P, K], BF16, align_bytes=64)
                grouped[n] = v_grouped
            rows = slice(quarter * QUARTER_ROWS, (quarter + 1) * QUARTER_ROWS)
            nc.scalar.copy(
                out=grouped[n][:].bitcast(F32).rearrange("c (g r w) -> c g r w", g=PASSES, w=2)[
                    :, :, rows, :
                ],
                in_=v_t[:].bitcast(F32).rearrange("c (r g w) -> c g r w", g=PASSES, w=2),
            )

        def quantise_weights():
            for g in range(PASSES):
                nc.vector.tensor_copy(
                    out=wc_grouped[:, g].rearrange("c (m i) t -> c m t i", i=4),
                    in_=wc_raw[:, g].rearrange("c t (m i) -> c m t i", i=4),
                )
            half = PASSES // 2
            for h in range(2):
                cols = slice(h * half * N_OUT, (h + 1) * half * N_OUT)
                nc.vector.quantize_mx(
                    out=wc_codes[:, cols].bitcast(FP8X4),
                    scales=wc_scales[:, cols],
                    in_=wc_grouped[:, h * half : (h + 1) * half].rearrange("c g n t -> c (g n t)"),
                )

        def quantise_and_contract(n, pair):
            v_codes = code_pool.tile([P, PAIR * P], U32, align_bytes=64)
            v_scales = code_pool.tile([P, PAIR * P], U8, align_bytes=64)
            nc.vector.quantize_mx(
                out=v_codes[:].bitcast(FP8X4),
                scales=v_scales[:],
                in_=grouped[n][:, pair * PAIR * K_PASS : (pair + 1) * PAIR * K_PASS],
            )
            if pair == 0:
                acc = psum_acc.tile([P, N_OUT], F32)
                accs[n] = acc
            for gg in range(PAIR):
                g = pair * PAIR + gg
                nc.tensor.matmul_mx(
                    out=accs[n][:],
                    lhsT=v_codes[:, gg * P : (gg + 1) * P].bitcast(FP8X4),
                    lhsT_scale=v_scales[:, gg * P : (gg + 1) * P],
                    rhs=wc_codes[:, g * N_OUT : (g + 1) * N_OUT].bitcast(FP8X4),
                    rhs_scale=wc_scales[:, g * N_OUT : (g + 1) * N_OUT],
                    start=(g == 0),
                    stop=(g == PASSES - 1),
                )

        def finish(n):
            res = res_pool.tile([P, N_OUT], F32)
            nc.vector.tensor_tensor(out=res[:], in0=accs[n][:], in1=bias_rows[:], op=ALU.add)
            nc.sync.dma_start(out=out[n * P : (n + 1) * P, :], in_=res[:])

        for n in range(LEAD):
            for quarter in range(QUARTERS):
                square_and_fold(n, quarter)
        for k in range(BATCH_TILES + 2):
            squaring = k + LEAD < BATCH_TILES
            reducing = k < BATCH_TILES
            b = k - 1
            contracting = 0 <= b < BATCH_TILES

            if squaring:
                square_and_fold(k + LEAD, 0)
                square_and_fold(k + LEAD, 1)
            if reducing:
                reduce_capsules(k)
                one_plus_squared(k)
            if squaring:
                square_and_fold(k + LEAD, 2)
            if contracting:
                for quarter in range(QUARTERS - 1):
                    multiply(b, quarter)
                    transpose(b, quarter)
                multiply(b, QUARTERS - 1)
            if reducing:
                radicand(k)
                seed(k)
            if contracting:
                transpose(b, QUARTERS - 1)
            if squaring:
                square_and_fold(k + LEAD, 3)
            if b == 0:
                quantise_weights()
            if k >= 2:
                finish(k - 2)
            if reducing:
                make_factor(k)
            if contracting:
                for pair in range(PASSES // PAIR):
                    quantise_and_contract(b, pair)
